import numpy as np
import ml_dtypes


def mxq(x, axis, fmt="e4m3"):
    dtype, down = {"e4m3": (ml_dtypes.float8_e4m3fn, 7), "e5m2": (ml_dtypes.float8_e5m2, 14)}[fmt]
    v = np.moveaxis(np.asarray(x, np.float32).astype(ml_dtypes.bfloat16).astype(np.float64), axis, -1)
    blocks = v.reshape(v.shape[:-1] + (-1, 32))
    amax = np.abs(blocks).max(-1, keepdims=True)
    byte = np.maximum(np.where(amax > 0, np.frexp(amax)[1] - 1 + 127, 0) - down, 1)
    scale = np.exp2(byte - 127.0)
    codes = (blocks / scale).astype(np.float32).astype(dtype).astype(np.float64)
    return np.moveaxis((codes * scale).reshape(v.shape), -1, axis)


WIDE = False


def mx_kscale(k):
    if not WIDE:
        return np.ones(k)
    levels = np.array([18, -18])
    if k % 512:
        return np.exp2(np.random.permutation(np.resize(levels, k // 32))).repeat(32)
    a = np.empty((k // 512, 16))
    for p in range(k // 512):
        a[p, :8] = np.random.permutation(np.resize(levels, 8))
        for g in range(8):
            far = levels[np.abs(levels - a[p, g]) >= 10]
            a[p, g + 8] = far[np.random.randint(len(far))]
    return np.exp2(a.ravel()).repeat(32)


BF16 = ml_dtypes.bfloat16


def bf(x):
    return np.asarray(x, np.float32).astype(BF16)


def f64(x):
    return np.asarray(x).astype(np.float64)


N, T, C, D, H, DO = 4, 256, 1024, 1024, 16, 1024
HD = D // H


def head_scores(q, k):
    return np.stack([(q * k[:, :, g:g + 1, :]).sum(-1) for g in range(H)], axis=-1)


def softmax(s):
    e = np.exp(s - s.max(-1, keepdims=True))
    return e / e.sum(-1, keepdims=True)


def setup_inputs():
    s = mx_kscale(N * T).reshape(N, T, 1)
    u = mx_kscale(2 * D)
    uq = u[:D:HD]
    x0 = bf(np.random.standard_normal((N, T, C)))
    w0 = bf(np.random.standard_normal((C, 2 * D)) / np.sqrt(C))
    b_qk = bf(np.random.standard_normal(2 * D) * 0.3)
    g = np.random.standard_normal((N, T, H, H)) * np.exp2(np.random.randint(-6, 1, (N, T, 1, 1))) * 16.0
    qk = f64(x0) @ f64(w0) + f64(b_qk)
    qh = qk.reshape(N, T, 2, H, HD)
    attn = softmax(head_scores(qh[:, :, 0] * HD ** -0.5, qh[:, :, 1]))
    uw = np.concatenate([np.repeat(uq, HD), uq.max() * u[D:] ** 0.2])
    return {"x": bf(f64(x0) * s),
            "w_qk": bf(f64(w0) / uw),
            "b_qk": b_qk,
            "qk": np.asarray(qk, np.float32),
            "attn": np.asarray(attn, np.float32),
            "grad_out": bf(g / s[..., None] * uq[:, None])}


def reference(x, w_qk, b_qk, qk, attn, grad_out):
    qh = f64(qk).reshape(N, T, 2, H, HD)
    q, k = qh[:, :, 0], qh[:, :, 1]
    a, g = f64(attn), f64(grad_out)
    ds = a * (g - (g * a).sum(-1, keepdims=True)) * HD ** -0.5
    dq = np.stack([(ds[:, :, h, :, None] * k).sum(2) for h in range(H)], axis=2)
    dk = np.stack([(ds[:, :, :, j, None] * q).sum(2) for j in range(H)], axis=2)
    dqk = np.concatenate([dq.reshape(N * T, D), dk.reshape(N * T, D)], axis=1)
    xf = f64(x).reshape(N * T, C)
    dx = mxq(dqk, 1, "e5m2") @ mxq(f64(w_qk), 1, "e4m3").T
    dw = mxq(xf, 0, "e4m3").T @ mxq(dqk, 0, "e5m2")
    return dx.reshape(N, T, C), dw

@@ -1,0 +1,371 @@
+from contextlib import ExitStack
+
+import concourse.mybir as mybir
+from concourse.masks import make_identity
+
+F32 = mybir.dt.float32
+BF16 = mybir.dt.bfloat16
+U32 = mybir.dt.uint32
+U8 = mybir.dt.uint8
+E4M3 = mybir.dt.float8_e4m3fn_x4
+E5M2 = mybir.dt.float8_e5m2_x4
+ALU = mybir.AluOpType
+AX = mybir.AxisListType
+
+P = 128
+FLOPS = 2 * (2 * 1024 * 1024 * 2048) + 2 * (2 * 1024 * 16 * 16 * 64)
+
+
+def tile_attention_pa_v_kernel(tc, x, w_qk, b_qk, qk, attn, grad_out, out_0, out_1):
+    nc = tc.nc
+
+    x_v = x.rearrange("n t c -> (n t) c").rearrange("(h p j) c -> h p j c", h=2, j=4)
+    w_v = w_qk.rearrange("(i c) f -> i c f", c=P)
+    qk_v = qk.rearrange("n t f -> (n t) f").rearrange("(h a q t) (r d) -> h t a r q d", h=2, a=4, q=32, t=4, d=64)
+    at_v = attn.rearrange("n t h g -> (n t) (h g)").rearrange("(h p t) f -> h p t f", h=2, t=4)
+    go_v = grad_out.rearrange("n t h g -> (n t) (h g)").rearrange("(h p t) f -> h p t f", h=2, t=4)
+    o0_v = out_0.rearrange("n t c -> (n t) c").rearrange("(h p t) c -> h t p c", h=2, t=4)
+
+    with ExitStack() as ctx:
+        const = ctx.enter_context(tc.tile_pool(name="const", bufs=1))
+        big = ctx.enter_context(tc.tile_pool(name="big", bufs=8))
+        work = ctx.enter_context(tc.tile_pool(name="work", bufs=2))
+        keep = ctx.enter_context(tc.tile_pool(name="keep", bufs=1))
+        ps_a = ctx.enter_context(tc.psum_pool(name="ps_a", bufs=3))
+        ps_t = ctx.enter_context(tc.psum_pool(name="ps_t", bufs=2))
+        ps_o = ctx.enter_context(tc.psum_pool(name="ps_o", bufs=3))
+
+        ident = const.tile([P, P], F32, name="ident", align_bytes=64)
+        make_identity(nc, ident[:])
+        blk = const.tile([P, 8], F32, name="blk")
+        nc.vector.tensor_reduce(out=blk[:], in_=ident[:].rearrange("p (c x) -> p c x", x=16), axis=AX.X, op=ALU.add)
+
+        w_codes = keep.tile([P, 4, 1024], U32, name="w_codes", align_bytes=64)
+        w_scales = keep.tile([P, 4, 1024], U8, name="w_scales", align_bytes=64)
+        x_codes = keep.tile([P, 2, 1024], U32, name="x_codes", align_bytes=64)
+        x_scales = keep.tile([P, 2, 1024], U8, name="x_scales", align_bytes=64)
+        t_codes = keep.tile([P, 2, 2048], U32, name="t_codes", align_bytes=64)
+        t_scales = keep.tile([P, 2, 2048], U8, name="t_scales", align_bytes=64)
+
+        def big_tile(name):
+            return big.tile([P, 2048], F32, name=name, tag="big", align_bytes=64)
+
+        at = {}
+        go = {}
+        kq = {}
+        wr = {}
+        xr = {}
+
+        def load_attn(h):
+            at[h] = work.tile([P, 4, 256], F32, name="at", tag="at", bufs=1)
+            go[h] = work.tile([P, 4, 256], BF16, name="go", tag="go", bufs=1)
+            nc.sync.dma_start(out=at[h][:], in_=at_v[h])
+            nc.sync.dma_start(out=go[h][:], in_=go_v[h])
+
+        def load_kq(h, t):
+            kq[h, t] = big_tile("kq")
+            for a in range(4):
+                nc.sync.dma_start(
+                    out=kq[h, t][32 * a : 32 * a + 32, :].rearrange("r (q d) -> r q d", d=64),
+                    in_=qk_v[h, t, a],
+                )
+
+        def load_w(i2):
+            tile = big_tile("wr")
+            for k in range(2):
+                nc.sync.dma_start(
+                    out=tile[:, 1024 * k : 1024 * (k + 1)].bitcast(BF16),
+                    in_=w_v[2 * i2 + k],
+                )
+            wr[i2] = tile
+
+        def load_x(h):
+            xr[h] = big_tile("xr")
+            nc.sync.dma_start(
+                out=xr[h][:].bitcast(BF16).rearrange("p (j c) -> p j c", j=4),
+                in_=x_v[h],
+            )
+
+        wg = {}
+
+        def w_turn(half, i):
+            c_tile = 4 * half + i
+            for gp in range(2):
+                if i == 0:
+                    wg[half, gp] = big_tile("wg")
+                pt = ps_t.tile([P, 4, P], F32, name="pt", tag="pt")
+                for k in range(4):
+                    g, u = 2 * gp + k // 2, k % 2
+                    src = wr[c_tile // 2][:, 1024 * (c_tile % 2) + 256 * g + u : 1024 * (c_tile % 2) + 256 * (g + 1) : 2]
+                    nc.tensor.transpose(pt[:, k, :], src, ident[:])
+                nc.scalar.copy(
+                    out=wg[half, gp][:].rearrange("p (g c u) -> p g c u", g=2, u=2)[:, :, P * i : P * (i + 1), :],
+                    in_=pt[:].rearrange("p (g u) c -> p g c u", u=2),
+                )
+
+        def w_quant(half):
+            for g in range(4):
+                nc.vector.quantize_mx(
+                    out=w_codes[:, g, 512 * half : 512 * (half + 1)].bitcast(E4M3),
+                    scales=w_scales[:, g, 512 * half : 512 * (half + 1)],
+                    in_=wg[half, g // 2][:, 1024 * (g % 2) : 1024 * (g % 2 + 1)].bitcast(BF16),
+                )
+
+        xi = {}
+
+        def x_mix(h, q):
+            if q == 0:
+                xi[h] = big_tile("xi")
+            nc.scalar.copy(
+                out=xi[h][:].bitcast(BF16).rearrange("p (c j) -> p c j", j=4)[:, 512 * q : 512 * (q + 1)],
+                in_=xr[h][:].bitcast(BF16).rearrange("p (j c) -> p c j", j=4)[:, 512 * q : 512 * (q + 1)],
+            )
+
+        def x_quant(h, q):
+            nc.vector.quantize_mx(
+                out=x_codes[:, h, 512 * q : 512 * (q + 1)].bitcast(E4M3),
+                scales=x_scales[:, h, 512 * q : 512 * (q + 1)],
+                in_=xi[h][:, 1024 * q : 1024 * (q + 1)].bitcast(BF16),
+            )
+
+        sr = {}
+
+        def ds(h, t0, nt):
+            n = 256 * nt
+            tmp = work.tile([P, 512], F32, name="tmp", tag="tmp", bufs=2)
+            r = work.tile([P, 64], F32, name="r", tag="r", bufs=2)
+            g2 = work.tile([P, 2, 16, 2, 16], F32, name="g2", tag="g2", bufs=1, align_bytes=64)
+            a_s = at[h][:, t0 : t0 + nt, :].rearrange("p t f -> p (t f)")
+            g_s = go[h][:, t0 : t0 + nt, :].rearrange("p t f -> p (t f)")
+            nc.vector.tensor_tensor(out=tmp[:, :n], in0=g_s, in1=a_s, op=ALU.mult)
+            nc.vector.tensor_reduce(
+                out=r[:, : 16 * nt], in_=tmp[:, :n].rearrange("p (m g) -> p m g", g=16), axis=AX.X, op=ALU.add
+            )
+            df = work.tile([P, 512], F32, name="df", tag="tmp", bufs=2)
+            nc.vector.tensor_tensor(
+                out=df[:, :n].rearrange("p (m g) -> p m g", g=16),
+                in0=g_s.rearrange("p (m g) -> p m g", g=16),
+                in1=r[:, : 16 * nt].unsqueeze(2).to_broadcast([P, 16 * nt, 16]),
+                op=ALU.subtract,
+            )
+            nat = g2[:, 0:nt, :, 1, :]
+            nc.vector.scalar_tensor_tensor(
+                out=nat.rearrange("p t j x -> p (t j) x"),
+                in0=df[:, :n].rearrange("p (m g) -> p m g", g=16),
+                scalar=0.125,
+                in1=a_s.rearrange("p (m g) -> p m g", g=16),
+                op0=ALU.mult,
+                op1=ALU.mult,
+            )
+            nc.scalar.copy(out=g2[:, 0:nt, :, 0, :], in_=nat.rearrange("p t j x -> p t x j"))
+            for t in range(nt):
+                sr[h, t0 + t] = work.tile([P, 16, 32], F32, name="sr", tag="sr", bufs=6, align_bytes=64)
+                nc.vector.transpose(
+                    out=sr[h, t0 + t][:].rearrange("p j q -> p (j q)"),
+                    in_=g2[:, t].rearrange("p j s x -> p (j s x)"),
+                )
+
+        bd = {}
+
+        def spread(h, t, c0=0, c1=8):
+            if c0 == 0:
+                bd[h, t] = work.tile([P, 32, P], F32, name="bd", tag="bd", bufs=2, align_bytes=64)
+            for c in range(c0, c1):
+                a, s = c // 2, c % 2
+                nc.vector.tensor_scalar(
+                    out=bd[h, t][:, :, 16 * c : 16 * c + 16],
+                    in0=sr[h, t][:].rearrange("p j q -> p q j"),
+                    scalar1=blk[:, 2 * a + 1 - s : 2 * a + 2 - s],
+                    scalar2=None,
+                    op0=ALU.mult,
+                )
+
+        y = {}
+
+        def product(h, t, b):
+            if b == 0:
+                y[h, t] = work.tile([P, 1024], F32, name="y", tag="y", bufs=2, align_bytes=64)
+            pa = ps_a.tile([P, 8, 64], F32, name="pa", tag="pa")
+            for i in range(8):
+                q = 8 * b + i
+                nc.tensor.matmul(
+                    pa[:, i, :],
+                    lhsT=bd[h, t][:, q, :],
+                    rhs=kq[h, t][:, 64 * q : 64 * q + 64],
+                    start=True,
+                    stop=True,
+                )
+            nc.scalar.copy(
+                out=y[h, t][:].bitcast(BF16).rearrange("p (d q e) -> p d q e", d=32, e=2)[:, :, 8 * b : 8 * b + 8, :],
+                in_=pa[:].rearrange("p q (d e) -> p d q e", e=2),
+            )
+
+        ut = {}
+
+        def turn(h, t):
+            if t == 0:
+                ut[h] = work.tile([P, 4, 2, 32, 16], F32, name="ut", tag="ut", bufs=1, align_bytes=64)
+            yt = work.tile([P, 1024], F32, name="yt", tag="yt", bufs=2, align_bytes=64)
+            nc.vector.transpose(out=yt[:], in_=y[h, t][:])
+            nc.vector.tensor_copy(
+                out=ut[h][:, t],
+                in_=yt[:].rearrange("p (d u m) -> p u m d", u=2, m=32),
+            )
+
+        fq = {}
+
+        def feat_turn(h, t):
+            fq[h, t] = work.tile([P, 4, P, 2], F32, name="fq", tag="fq", bufs=2, align_bytes=64)
+            for gp in range(2):
+                pt = ps_t.tile([P, 4, P], F32, name="pt", tag="pt")
+                for k in range(4):
+                    g, u = 2 * gp + k // 2, k % 2
+                    nc.tensor.transpose(
+                        pt[:, k, :],
+                        ut[h][:, t, u, 8 * g : 8 * g + 8, :].rearrange("p m d -> p (m d)"),
+                        ident[:],
+                    )
+                nc.scalar.copy(
+                    out=fq[h, t][:, 2 * gp : 2 * gp + 2],
+                    in_=pt[:].rearrange("p (g u) c -> p g c u", u=2),
+                )
+
+        fc = {}
+
+        def feat_quant(h, t):
+            codes = work.tile([P, 512], U32, name="f_codes", tag="f_codes", bufs=2, align_bytes=64)
+            scales = work.tile([P, 512], U8, name="f_scales", tag="f_scales", bufs=2, align_bytes=64)
+            nc.vector.quantize_mx(
+                out=codes[:].bitcast(E5M2),
+                scales=scales[:],
+                in_=fq[h, t][:].rearrange("p g c u -> p (g c u)").bitcast(BF16),
+            )
+            fc[h, t] = codes, scales
+
+        def dx(h, t):
+            codes, scales = fc[h, t]
+            o0 = work.tile([P, 1024], F32, name="o0", tag="o0", bufs=2)
+            for n in range(2):
+                po = ps_o.tile([P, 512], F32, name="po", tag="po")
+                for g in range(4):
+                    nc.tensor.matmul_mx(
+                        out=po[:],
+                        lhsT=codes[:, P * g : P * (g + 1)].bitcast(E5M2),
+                        lhsT_scale=scales[:, P * g : P * (g + 1)],
+                        rhs=w_codes[:, g, 512 * n : 512 * (n + 1)].bitcast(E4M3),
+                        rhs_scale=w_scales[:, g, 512 * n : 512 * (n + 1)],
+                        start=(g == 0),
+                        stop=(g == 3),
+                    )
+                nc.scalar.copy(out=o0[:, 512 * n : 512 * (n + 1)], in_=po[:])
+            nc.scalar.dma_start(out=o0_v[h, t], in_=o0[:])
+
+        def tok_quant(h, g):
+            z = work.tile([P, 2, 256, 4], BF16, name="z", tag="z", bufs=2, align_bytes=64)
+            nc.vector.tensor_copy(
+                out=z[:],
+                in_=ut[h][:].rearrange("p t u m d -> p (t u m d)").bitcast(BF16)
+                .rearrange("p (t u g w) -> p g u w t", t=4, u=2, g=4)[:, g],
+            )
+            nc.vector.quantize_mx(
+                out=t_codes[:, h, 512 * g : 512 * (g + 1)].bitcast(E5M2),
+                scales=t_scales[:, h, 512 * g : 512 * (g + 1)],
+                in_=z[:].rearrange("p u w t -> p (u w t)"),
+            )
+
+        def dw(m):
+            o1 = big_tile("o1")
+            for g in range(4):
+                if g % 2 == 0:
+                    po = ps_o.tile([P, 512], F32, name="po", tag="po")
+                else:
+                    po = ps_a.tile([P, 512], F32, name="pa", tag="pa")
+                for h in range(2):
+                    nc.tensor.matmul_mx(
+                        out=po[:],
+                        lhsT=x_codes[:, h, P * m : P * (m + 1)].bitcast(E4M3),
+                        lhsT_scale=x_scales[:, h, P * m : P * (m + 1)],
+                        rhs=t_codes[:, h, 512 * g : 512 * (g + 1)].bitcast(E5M2),
+                        rhs_scale=t_scales[:, h, 512 * g : 512 * (g + 1)],
+                        start=(h == 0),
+                        stop=(h == 1),
+                    )
+                dst = o1[:, 512 * g : 512 * (g + 1)].rearrange("p (w u e) -> p w u e", u=2, e=2)
+                src = po[:].rearrange("p (u w e) -> p w u e", u=2, e=2)
+                if g % 2 == 0:
+                    nc.vector.tensor_copy(out=dst, in_=src)
+                else:
+                    nc.scalar.copy(out=dst, in_=src)
+                    cols = slice(512 * (g - 1), 512 * (g + 1))
+                    nc.sync.dma_start(out=out_1[P * m : P * (m + 1), cols], in_=o1[:, cols])
+
+        steps = [(h, t) for h in range(2) for t in range(4)]
+
+        load_attn(0)
+        load_w(0)
+        load_w(1)
+        load_kq(0, 0)
+        load_w(2)
+        load_w(3)
+        load_kq(0, 1)
+
+        with tc.manual_schedule():
+            ds(0, 0, 1)
+            spread(0, 0)
+            for i in range(4):
+                w_turn(0, i)
+            ds(0, 1, 1)
+            for n in range(10):
+                here = steps[n] if n < 8 else None
+                prev = steps[n - 1] if 1 <= n <= 8 else None
+                last = steps[n - 2] if 2 <= n <= 9 else None
+                if n == 1:
+                    load_attn(1)
+                if n + 2 < 8:
+                    load_kq(*steps[n + 2])
+                if n == 3 or n == 4:
+                    load_x(n - 3)
+                if prev:
+                    turn(*prev)
+                if here:
+                    product(*here, 0)
+                    product(*here, 1)
+                    if n + 1 < 8:
+                        spread(*steps[n + 1])
+                    product(*here, 2)
+                if n == 0:
+                    w_quant(0)
+                if n < 2:
+                    w_turn(1, 2 * n)
+                    w_turn(1, 2 * n + 1)
+                if n == 1:
+                    w_quant(1)
+                if n == 0:
+                    ds(0, 2, 2)
+                if n == 2 or n == 3:
+                    ds(1, 2 * (n - 2), 2)
+                if n == 4 or n == 8:
+                    tok_quant(n // 4 - 1, 0)
+                if n == 8 and last:
+                    dx(*last)
+                if prev:
+                    feat_turn(*prev)
+                if last and n < 8:
+                    dx(*last)
+                if here:
+                    product(*here, 3)
+                if prev:
+                    feat_quant(*prev)
+                if n == 9:
+                    dx(*last)
+                if n == 4 or n == 8:
+                    for g in range(1, 4):
+                        tok_quant(n // 4 - 1, g)
+                if n == 4 or n == 5:
+                    for q in range(2):
+                        x_mix(n - 4, q)
+                if n == 5 or n == 6:
+                    for q in range(2):
+                        x_quant(n - 5, q)
+            for m in range(8):
+                dw(m)

@@ -11,6 +11,7 @@ E4M3 = mybir.dt.float8_e4m3fn_x4
 E5M2 = mybir.dt.float8_e5m2_x4
 ALU = mybir.AluOpType
 AX = mybir.AxisListType
+ACT = mybir.ActivationFunctionType
 
 P = 128
 FLOPS = 2 * (2 * 1024 * 1024 * 2048) + 2 * (2 * 1024 * 16 * 16 * 64)
@@ -28,7 +29,7 @@ def tile_attention_pa_v_kernel(tc, x, w_qk, b_qk, qk, attn, grad_out, out_0, out
 
     with ExitStack() as ctx:
         const = ctx.enter_context(tc.tile_pool(name="const", bufs=1))
-        big = ctx.enter_context(tc.tile_pool(name="big", bufs=8))
+        big = ctx.enter_context(tc.tile_pool(name="big", bufs=7))
         work = ctx.enter_context(tc.tile_pool(name="work", bufs=2))
         keep = ctx.enter_context(tc.tile_pool(name="keep", bufs=1))
         ps_a = ctx.enter_context(tc.psum_pool(name="ps_a", bufs=3))
@@ -56,11 +57,12 @@ def tile_attention_pa_v_kernel(tc, x, w_qk, b_qk, qk, attn, grad_out, out_0, out
         wr = {}
         xr = {}
 
-        def load_attn(h):
-            at[h] = work.tile([P, 4, 256], F32, name="at", tag="at", bufs=1)
-            go[h] = work.tile([P, 4, 256], BF16, name="go", tag="go", bufs=1)
-            nc.sync.dma_start(out=at[h][:], in_=at_v[h])
-            nc.sync.dma_start(out=go[h][:], in_=go_v[h])
+        def load_attn(h, t0, t1):
+            if t0 == 0:
+                at[h] = work.tile([P, 4, 256], F32, name="at", tag="at", bufs=2)
+                go[h] = work.tile([P, 4, 256], BF16, name="go", tag="go", bufs=2)
+            nc.sync.dma_start(out=at[h][:, t0:t1, :], in_=at_v[h][:, t0:t1, :])
+            nc.sync.dma_start(out=go[h][:, t0:t1, :], in_=go_v[h][:, t0:t1, :])
 
         def load_kq(h, t):
             kq[h, t] = big_tile("kq")
@@ -116,7 +118,7 @@ def tile_attention_pa_v_kernel(tc, x, w_qk, b_qk, qk, attn, grad_out, out_0, out
         def x_mix(h, q):
             if q == 0:
                 xi[h] = big_tile("xi")
-            nc.scalar.copy(
+            nc.vector.tensor_copy(
                 out=xi[h][:].bitcast(BF16).rearrange("p (c j) -> p c j", j=4)[:, 512 * q : 512 * (q + 1)],
                 in_=xr[h][:].bitcast(BF16).rearrange("p (j c) -> p c j", j=4)[:, 512 * q : 512 * (q + 1)],
             )
@@ -129,56 +131,47 @@ def tile_attention_pa_v_kernel(tc, x, w_qk, b_qk, qk, attn, grad_out, out_0, out
             )
 
         sr = {}
+        turned_of = {}
 
-        def ds(h, t0, nt):
-            n = 256 * nt
-            tmp = work.tile([P, 512], F32, name="tmp", tag="tmp", bufs=2)
-            r = work.tile([P, 64], F32, name="r", tag="r", bufs=2)
-            g2 = work.tile([P, 2, 16, 2, 16], F32, name="g2", tag="g2", bufs=1, align_bytes=64)
-            a_s = at[h][:, t0 : t0 + nt, :].rearrange("p t f -> p (t f)")
-            g_s = go[h][:, t0 : t0 + nt, :].rearrange("p t f -> p (t f)")
-            nc.vector.tensor_tensor(out=tmp[:, :n], in0=g_s, in1=a_s, op=ALU.mult)
-            nc.vector.tensor_reduce(
-                out=r[:, : 16 * nt], in_=tmp[:, :n].rearrange("p (m g) -> p m g", g=16), axis=AX.X, op=ALU.add
-            )
-            df = work.tile([P, 512], F32, name="df", tag="tmp", bufs=2)
-            nc.vector.tensor_tensor(
-                out=df[:, :n].rearrange("p (m g) -> p m g", g=16),
-                in0=g_s.rearrange("p (m g) -> p m g", g=16),
-                in1=r[:, : 16 * nt].unsqueeze(2).to_broadcast([P, 16 * nt, 16]),
-                op=ALU.subtract,
-            )
-            nat = g2[:, 0:nt, :, 1, :]
-            nc.vector.scalar_tensor_tensor(
-                out=nat.rearrange("p t j x -> p (t j) x"),
-                in0=df[:, :n].rearrange("p (m g) -> p m g", g=16),
-                scalar=0.125,
-                in1=a_s.rearrange("p (m g) -> p m g", g=16),
-                op0=ALU.mult,
-                op1=ALU.mult,
-            )
-            nc.scalar.copy(out=g2[:, 0:nt, :, 0, :], in_=nat.rearrange("p t j x -> p t x j"))
-            for t in range(nt):
-                sr[h, t0 + t] = work.tile([P, 16, 32], F32, name="sr", tag="sr", bufs=6, align_bytes=64)
-                nc.vector.transpose(
-                    out=sr[h, t0 + t][:].rearrange("p j q -> p (j q)"),
-                    in_=g2[:, t].rearrange("p j s x -> p (j s x)"),
-                )
+        def ds_ops(h, t):
+            tmp = work.tile([P, 16, 16], F32, name="tmp", tag="tmp", bufs=2)
+            r = work.tile([P, 16], F32, name="r", tag="r", bufs=2)
+            df = work.tile([P, 16, 16], F32, name="df", tag="df", bufs=2)
+            g2 = work.tile([P, 16, 2, 16], F32, name="g2", tag="g2", bufs=2, align_bytes=64)
+            turned_of[h, t] = work.tile([P, 16, 32], F32, name="turned", tag="turned", bufs=2, align_bytes=64)
+            a_s = at[h][:, t, :].rearrange("p (m g) -> p m g", g=16)
+            g_s = go[h][:, t, :].rearrange("p (m g) -> p m g", g=16)
+            return [
+                lambda: nc.vector.tensor_tensor(out=tmp[:], in0=g_s, in1=a_s, op=ALU.mult),
+                lambda: nc.vector.tensor_reduce(out=r[:], in_=tmp[:], axis=AX.X, op=ALU.add),
+                lambda: nc.vector.tensor_tensor(
+                    out=df[:], in0=g_s, in1=r[:].unsqueeze(2).to_broadcast([P, 16, 16]), op=ALU.subtract
+                ),
+                lambda: nc.vector.scalar_tensor_tensor(
+                    out=g2[:, :, 1, :], in0=df[:], scalar=0.125, in1=a_s, op0=ALU.mult, op1=ALU.mult
+                ),
+                lambda: nc.vector.tensor_copy(out=g2[:, :, 0, :], in_=g2[:, :, 1, :].rearrange("p j x -> p x j")),
+                lambda: nc.vector.transpose(
+                    out=turned_of[h, t][:].rearrange("p j q -> p (j q)"), in_=g2[:].rearrange("p j s x -> p (j s x)")
+                ),
+            ]
+
+        def ds_sort(h, t):
+            sr[h, t] = work.tile([P, 32, 16], F32, name="sr", tag="sr", bufs=4)
+            nc.scalar.copy(out=sr[h, t][:], in_=turned_of[h, t][:].rearrange("p j q -> p q j"))
 
         bd = {}
 
-        def spread(h, t, c0=0, c1=8):
-            if c0 == 0:
+        def spread(h, t, c, on_scalar=False):
+            if c == 0:
                 bd[h, t] = work.tile([P, 32, P], F32, name="bd", tag="bd", bufs=2, align_bytes=64)
-            for c in range(c0, c1):
-                a, s = c // 2, c % 2
-                nc.vector.tensor_scalar(
-                    out=bd[h, t][:, :, 16 * c : 16 * c + 16],
-                    in0=sr[h, t][:].rearrange("p j q -> p q j"),
-                    scalar1=blk[:, 2 * a + 1 - s : 2 * a + 2 - s],
-                    scalar2=None,
-                    op0=ALU.mult,
-                )
+            a, s = c // 2, c % 2
+            out = bd[h, t][:, :, 16 * c : 16 * c + 16]
+            mask = blk[:, 2 * a + 1 - s : 2 * a + 2 - s]
+            if on_scalar:
+                nc.scalar.activation(out=out, in_=sr[h, t][:], func=ACT.Copy, scale=mask)
+            else:
+                nc.vector.tensor_scalar(out=out, in0=sr[h, t][:], scalar1=mask, scalar2=None, op0=ALU.mult)
 
         y = {}
 
@@ -201,16 +194,20 @@ def tile_attention_pa_v_kernel(tc, x, w_qk, b_qk, qk, attn, grad_out, out_0, out
             )
 
         ut = {}
+        yt = {}
 
         def turn(h, t):
             if t == 0:
                 ut[h] = work.tile([P, 4, 2, 32, 16], F32, name="ut", tag="ut", bufs=1, align_bytes=64)
-            yt = work.tile([P, 1024], F32, name="yt", tag="yt", bufs=2, align_bytes=64)
-            nc.vector.transpose(out=yt[:], in_=y[h, t][:])
-            nc.vector.tensor_copy(
-                out=ut[h][:, t],
-                in_=yt[:].rearrange("p (d u m) -> p u m d", u=2, m=32),
-            )
+            yt[h, t] = work.tile([P, 1024], F32, name="yt", tag="yt", bufs=1, align_bytes=64)
+            nc.vector.transpose(out=yt[h, t][:], in_=y[h, t][:])
+
+        def turn_sort(h, t):
+            for u in range(2):
+                nc.vector.tensor_copy(
+                    out=ut[h][:, t, u].rearrange("p (mm m) (dd d) -> p mm dd m d", m=4, d=4),
+                    in_=yt[h, t][:].rearrange("p (dd d u mm m) -> p u mm dd m d", dd=4, d=4, u=2, m=4)[:, u],
+                )
 
         fq = {}
 
@@ -233,8 +230,8 @@ def tile_attention_pa_v_kernel(tc, x, w_qk, b_qk, qk, attn, grad_out, out_0, out
         fc = {}
 
         def feat_quant(h, t):
-            codes = work.tile([P, 512], U32, name="f_codes", tag="f_codes", bufs=2, align_bytes=64)
-            scales = work.tile([P, 512], U8, name="f_scales", tag="f_scales", bufs=2, align_bytes=64)
+            codes = work.tile([P, 512], U32, name="f_codes", tag="f_codes", bufs=4, align_bytes=64)
+            scales = work.tile([P, 512], U8, name="f_scales", tag="f_scales", bufs=4, align_bytes=64)
             nc.vector.quantize_mx(
                 out=codes[:].bitcast(E5M2),
                 scales=scales[:],
@@ -244,7 +241,7 @@ def tile_attention_pa_v_kernel(tc, x, w_qk, b_qk, qk, attn, grad_out, out_0, out
 
         def dx(h, t):
             codes, scales = fc[h, t]
-            o0 = work.tile([P, 1024], F32, name="o0", tag="o0", bufs=2)
+            o0 = work.tile([P, 1024], F32, name="o0", tag="o0", bufs=3)
             for n in range(2):
                 po = ps_o.tile([P, 512], F32, name="po", tag="po")
                 for g in range(4):
@@ -260,23 +257,28 @@ def tile_attention_pa_v_kernel(tc, x, w_qk, b_qk, qk, attn, grad_out, out_0, out
                 nc.scalar.copy(out=o0[:, 512 * n : 512 * (n + 1)], in_=po[:])
             nc.scalar.dma_start(out=o0_v[h, t], in_=o0[:])
 
-        def tok_quant(h, g):
-            z = work.tile([P, 2, 256, 4], BF16, name="z", tag="z", bufs=2, align_bytes=64)
+        z = {}
+
+        def tok_mix(h, g):
+            z[h, g] = work.tile([P, 2, 256, 4], BF16, name="z", tag="z", bufs=2, align_bytes=64)
             nc.vector.tensor_copy(
-                out=z[:],
+                out=z[h, g][:],
                 in_=ut[h][:].rearrange("p t u m d -> p (t u m d)").bitcast(BF16)
                 .rearrange("p (t u g w) -> p g u w t", t=4, u=2, g=4)[:, g],
             )
+
+        def tok_quant(h, g):
             nc.vector.quantize_mx(
                 out=t_codes[:, h, 512 * g : 512 * (g + 1)].bitcast(E5M2),
                 scales=t_scales[:, h, 512 * g : 512 * (g + 1)],
-                in_=z[:].rearrange("p u w t -> p (u w t)"),
+                in_=z[h, g][:].rearrange("p u w t -> p (u w t)"),
             )
 
-        def dw(m):
+        def dw(m, gp):
             o1 = big_tile("o1")
-            for g in range(4):
-                if g % 2 == 0:
+            for k in range(2):
+                g = 2 * gp + k
+                if k == 0:
                     po = ps_o.tile([P, 512], F32, name="po", tag="po")
                 else:
                     po = ps_a.tile([P, 512], F32, name="pa", tag="pa")
@@ -290,82 +292,117 @@ def tile_attention_pa_v_kernel(tc, x, w_qk, b_qk, qk, attn, grad_out, out_0, out
                         start=(h == 0),
                         stop=(h == 1),
                     )
-                dst = o1[:, 512 * g : 512 * (g + 1)].rearrange("p (w u e) -> p w u e", u=2, e=2)
+                dst = o1[:, 512 * k : 512 * (k + 1)].rearrange("p (w u e) -> p w u e", u=2, e=2)
                 src = po[:].rearrange("p (u w e) -> p w u e", u=2, e=2)
-                if g % 2 == 0:
+                if k == 0:
                     nc.vector.tensor_copy(out=dst, in_=src)
                 else:
                     nc.scalar.copy(out=dst, in_=src)
-                    cols = slice(512 * (g - 1), 512 * (g + 1))
-                    nc.sync.dma_start(out=out_1[P * m : P * (m + 1), cols], in_=o1[:, cols])
+            nc.sync.dma_start(out=out_1[P * m : P * (m + 1), 1024 * gp : 1024 * (gp + 1)], in_=o1[:, 0:1024])
 
         steps = [(h, t) for h in range(2) for t in range(4)]
+        ds_at = {0: [2], 1: [3], 2: [4, 5], 3: [6], 5: [7]}
 
-        load_attn(0)
+        load_attn(0, 0, 1)
         load_w(0)
-        load_w(1)
         load_kq(0, 0)
+        load_attn(0, 1, 4)
+        load_w(1)
         load_w(2)
-        load_w(3)
         load_kq(0, 1)
+        load_attn(1, 0, 4)
 
         with tc.manual_schedule():
-            ds(0, 0, 1)
-            spread(0, 0)
-            for i in range(4):
-                w_turn(0, i)
-            ds(0, 1, 1)
-            for n in range(10):
-                here = steps[n] if n < 8 else None
-                prev = steps[n - 1] if 1 <= n <= 8 else None
-                last = steps[n - 2] if 2 <= n <= 9 else None
-                if n == 1:
-                    load_attn(1)
-                if n + 2 < 8:
+            for op in ds_ops(0, 0):
+                op()
+            w_turn(0, 0)
+            ds_sort(0, 0)
+            w_turn(0, 1)
+            load_w(3)
+            for c in range(8):
+                spread(0, 0, c)
+            for op in ds_ops(0, 1):
+                op()
+            for n in range(8):
+                here = steps[n]
+                after = steps[n + 1] if n < 7 else None
+                prev = steps[n - 1] if n > 0 else None
+                new = [steps[c] for c in ds_at.get(n, [])]
+                if 0 < n and n + 2 < 8:
                     load_kq(*steps[n + 2])
-                if n == 3 or n == 4:
-                    load_x(n - 3)
+                if n == 4 or n == 5:
+                    load_x(n - 4)
                 if prev:
                     turn(*prev)
-                if here:
-                    product(*here, 0)
-                    product(*here, 1)
-                    if n + 1 < 8:
-                        spread(*steps[n + 1])
-                    product(*here, 2)
+                product(*here, 0)
                 if n == 0:
-                    w_quant(0)
+                    ds_sort(0, 1)
+                if after:
+                    spread(*after, 0)
+                    spread(*after, 1)
+                if prev:
+                    turn_sort(*prev)
+                product(*here, 1)
+                todo = [op for c in new for op in ds_ops(*c)]
+                each = len(todo) // 6
+                if n == 4:
+                    tok_mix(0, 0)
+                    tok_mix(0, 1)
+                    tok_quant(0, 0)
+                for c in range(2, 8):
+                    if after:
+                        spread(*after, c, c >= 6 and 2 <= n <= 3 or c >= 5 and n == 4)
+                    if n == 4 and c < 4:
+                        tok_mix(0, c)
+                        tok_quant(0, c - 1)
+                    if n == 4 and c == 4:
+                        tok_quant(0, 3)
+                    for op in todo[each * (c - 2) : each * (c - 1)]:
+                        op()
+                product(*here, 2)
                 if n < 2:
-                    w_turn(1, 2 * n)
-                    w_turn(1, 2 * n + 1)
-                if n == 1:
-                    w_quant(1)
+                    w_turn(n, 2)
+                    w_turn(n, 3)
+                    w_quant(n)
                 if n == 0:
-                    ds(0, 2, 2)
-                if n == 2 or n == 3:
-                    ds(1, 2 * (n - 2), 2)
-                if n == 4 or n == 8:
-                    tok_quant(n // 4 - 1, 0)
-                if n == 8 and last:
-                    dx(*last)
+                    load_kq(*steps[2])
+                    w_turn(1, 0)
+                    w_turn(1, 1)
                 if prev:
                     feat_turn(*prev)
-                if last and n < 8:
-                    dx(*last)
-                if here:
-                    product(*here, 3)
+                if 2 <= n < 6:
+                    dx(*steps[n - 2])
+                product(*here, 3)
                 if prev:
                     feat_quant(*prev)
-                if n == 9:
-                    dx(*last)
-                if n == 4 or n == 8:
-                    for g in range(1, 4):
-                        tok_quant(n // 4 - 1, g)
-                if n == 4 or n == 5:
+                for c in new:
+                    ds_sort(*c)
+                if n == 6 or n == 7:
                     for q in range(2):
-                        x_mix(n - 4, q)
-                if n == 5 or n == 6:
+                        x_mix(n - 6, q)
                     for q in range(2):
-                        x_quant(n - 5, q)
+                        x_quant(n - 6, q)
+            turn(*steps[7])
+            turn_sort(*steps[7])
+            dx(*steps[4])
+            dx(*steps[5])
+            tok_mix(1, 0)
+            tok_mix(1, 1)
+            tok_quant(1, 0)
+            tok_quant(1, 1)
+            feat_turn(*steps[7])
+            dx(*steps[6])
+            feat_quant(*steps[7])
+            dw(0, 0)
+            dw(1, 0)
+            tok_mix(1, 2)
+            tok_mix(1, 3)
+            tok_quant(1, 2)
+            tok_quant(1, 3)
+            dw(2, 0)
+            dw(3, 0)
+            dx(*steps[7])
+            for m in range(4, 8):
+                dw(m, 0)
             for m in range(8):
-                dw(m)
+                dw(m, 1)

@@ -118,9 +118,9 @@ def tile_attention_pa_v_kernel(tc, x, w_qk, b_qk, qk, attn, grad_out, out_0, out
         def x_mix(h, q):
             if q == 0:
                 xi[h] = big_tile("xi")
-            nc.vector.tensor_copy(
-                out=xi[h][:].bitcast(BF16).rearrange("p (c j) -> p c j", j=4)[:, 512 * q : 512 * (q + 1)],
-                in_=xr[h][:].bitcast(BF16).rearrange("p (j c) -> p c j", j=4)[:, 512 * q : 512 * (q + 1)],
+            nc.scalar.copy(
+                out=xi[h][:].bitcast(BF16).rearrange("p (c j) -> p c j", j=4)[:, 256 * q : 256 * (q + 1)],
+                in_=xr[h][:].bitcast(BF16).rearrange("p (j c) -> p c j", j=4)[:, 256 * q : 256 * (q + 1)],
             )
 
         def x_quant(h, q):
@@ -133,28 +133,36 @@ def tile_attention_pa_v_kernel(tc, x, w_qk, b_qk, qk, attn, grad_out, out_0, out
         sr = {}
         turned_of = {}
 
-        def ds_ops(h, t):
-            tmp = work.tile([P, 16, 16], F32, name="tmp", tag="tmp", bufs=2)
-            r = work.tile([P, 16], F32, name="r", tag="r", bufs=2)
-            df = work.tile([P, 16, 16], F32, name="df", tag="df", bufs=2)
-            g2 = work.tile([P, 16, 2, 16], F32, name="g2", tag="g2", bufs=2, align_bytes=64)
-            turned_of[h, t] = work.tile([P, 16, 32], F32, name="turned", tag="turned", bufs=2, align_bytes=64)
-            a_s = at[h][:, t, :].rearrange("p (m g) -> p m g", g=16)
-            g_s = go[h][:, t, :].rearrange("p (m g) -> p m g", g=16)
-            return [
-                lambda: nc.vector.tensor_tensor(out=tmp[:], in0=g_s, in1=a_s, op=ALU.mult),
-                lambda: nc.vector.tensor_reduce(out=r[:], in_=tmp[:], axis=AX.X, op=ALU.add),
+        def ds_ops(h, t0, nt):
+            m = 16 * nt
+            tmp = work.tile([P, 32, 16], F32, name="tmp", tag="tmp", bufs=2)
+            r = work.tile([P, 32], F32, name="r", tag="r", bufs=2)
+            df = work.tile([P, 32, 16], F32, name="df", tag="tmp", bufs=2)
+            g2 = work.tile([P, 2, 16, 2, 16], F32, name="g2", tag="g2", bufs=1, align_bytes=64)
+            for t in range(t0, t0 + nt):
+                turned_of[h, t] = work.tile([P, 16, 32], F32, name="turned", tag="turned", bufs=3, align_bytes=64)
+            a_s = at[h][:, t0 : t0 + nt, :].rearrange("p t (m g) -> p (t m) g", g=16)
+            g_s = go[h][:, t0 : t0 + nt, :].rearrange("p t (m g) -> p (t m) g", g=16)
+            nat = g2[:, :nt, :, 1, :]
+
+            def turn_ds(t):
+                nc.vector.transpose(
+                    out=turned_of[h, t][:].rearrange("p j q -> p (j q)"),
+                    in_=g2[:, t - t0].rearrange("p j s x -> p (j s x)"),
+                )
+
+            ops = [
+                lambda: nc.vector.tensor_tensor(out=tmp[:, :m], in0=g_s, in1=a_s, op=ALU.mult),
+                lambda: nc.vector.tensor_reduce(out=r[:, :m], in_=tmp[:, :m], axis=AX.X, op=ALU.add),
                 lambda: nc.vector.tensor_tensor(
-                    out=df[:], in0=g_s, in1=r[:].unsqueeze(2).to_broadcast([P, 16, 16]), op=ALU.subtract
+                    out=df[:, :m], in0=g_s, in1=r[:, :m].unsqueeze(2).to_broadcast([P, m, 16]), op=ALU.subtract
                 ),
                 lambda: nc.vector.scalar_tensor_tensor(
-                    out=g2[:, :, 1, :], in0=df[:], scalar=0.125, in1=a_s, op0=ALU.mult, op1=ALU.mult
+                    out=nat.rearrange("p t j x -> p (t j) x"), in0=df[:, :m], scalar=0.125, in1=a_s, op0=ALU.mult, op1=ALU.mult
                 ),
-                lambda: nc.vector.tensor_copy(out=g2[:, :, 0, :], in_=g2[:, :, 1, :].rearrange("p j x -> p x j")),
-                lambda: nc.vector.transpose(
-                    out=turned_of[h, t][:].rearrange("p j q -> p (j q)"), in_=g2[:].rearrange("p j s x -> p (j s x)")
-                ),
+                lambda: nc.vector.tensor_copy(out=g2[:, :nt, :, 0, :], in_=nat.rearrange("p t j x -> p t x j")),
             ]
+            return ops + [lambda t=t: turn_ds(t) for t in range(t0, t0 + nt)]
 
         def ds_sort(h, t):
             sr[h, t] = work.tile([P, 32, 16], F32, name="sr", tag="sr", bufs=4)
@@ -301,7 +309,9 @@ def tile_attention_pa_v_kernel(tc, x, w_qk, b_qk, qk, attn, grad_out, out_0, out
             nc.sync.dma_start(out=out_1[P * m : P * (m + 1), 1024 * gp : 1024 * (gp + 1)], in_=o1[:, 0:1024])
 
         steps = [(h, t) for h in range(2) for t in range(4)]
-        ds_at = {0: [2], 1: [3], 2: [4, 5], 3: [6], 5: [7]}
+        ds_at = {0: [(0, 2, 2)], 1: [(1, 0, 2)], 3: [(1, 2, 2)]}
+        sort_at = {0: [2], 1: [3], 2: [4, 5], 4: [6, 7]}
+        x_at = {3: [(0, 0), (0, 1)], 4: [(0, 2), (0, 3)], 5: [(1, 0), (1, 1)], 6: [(1, 2), (1, 3)]}
 
         load_attn(0, 0, 1)
         load_w(0)
@@ -313,7 +323,7 @@ def tile_attention_pa_v_kernel(tc, x, w_qk, b_qk, qk, attn, grad_out, out_0, out
         load_attn(1, 0, 4)
 
         with tc.manual_schedule():
-            for op in ds_ops(0, 0):
+            for op in ds_ops(0, 0, 1):
                 op()
             w_turn(0, 0)
             ds_sort(0, 0)
@@ -321,69 +331,71 @@ def tile_attention_pa_v_kernel(tc, x, w_qk, b_qk, qk, attn, grad_out, out_0, out
             load_w(3)
             for c in range(8):
                 spread(0, 0, c)
-            for op in ds_ops(0, 1):
+            for op in ds_ops(0, 1, 1):
                 op()
             for n in range(8):
                 here = steps[n]
                 after = steps[n + 1] if n < 7 else None
                 prev = steps[n - 1] if n > 0 else None
-                new = [steps[c] for c in ds_at.get(n, [])]
+                todo = [op for c in ds_at.get(n, []) for op in ds_ops(*c)]
                 if 0 < n and n + 2 < 8:
                     load_kq(*steps[n + 2])
-                if n == 4 or n == 5:
-                    load_x(n - 4)
+                if n == 2 or n == 4:
+                    load_x(n // 4)
                 if prev:
                     turn(*prev)
                 product(*here, 0)
                 if n == 0:
+                    product(*here, 1)
+                    w_turn(0, 2)
                     ds_sort(0, 1)
-                if after:
-                    spread(*after, 0)
-                    spread(*after, 1)
-                if prev:
-                    turn_sort(*prev)
-                product(*here, 1)
-                todo = [op for c in new for op in ds_ops(*c)]
-                each = len(todo) // 6
+                for c in range(8):
+                    if c == 2 and prev:
+                        turn_sort(*prev)
+                    if after:
+                        spread(*after, c, n > 1 and c >= 6)
+                    if c == 3 and n > 0:
+                        product(*here, 1)
+                    if todo and c >= 2 and n > 0:
+                        todo.pop(0)()
+                for op in todo:
+                    op()
+                if 2 <= n:
+                    feat_quant(*steps[n - 2])
                 if n == 4:
                     tok_mix(0, 0)
-                    tok_mix(0, 1)
-                    tok_quant(0, 0)
-                for c in range(2, 8):
-                    if after:
-                        spread(*after, c, c >= 6 and 2 <= n <= 3 or c >= 5 and n == 4)
-                    if n == 4 and c < 4:
-                        tok_mix(0, c)
-                        tok_quant(0, c - 1)
-                    if n == 4 and c == 4:
-                        tok_quant(0, 3)
-                    for op in todo[each * (c - 2) : each * (c - 1)]:
-                        op()
-                product(*here, 2)
-                if n < 2:
-                    w_turn(n, 2)
-                    w_turn(n, 3)
-                    w_quant(n)
+                    for g in range(1, 4):
+                        tok_mix(0, g)
+                        tok_quant(0, g - 1)
+                    tok_quant(0, 3)
                 if n == 0:
-                    load_kq(*steps[2])
+                    w_turn(0, 3)
+                if n == 1:
                     w_turn(1, 0)
                     w_turn(1, 1)
+                product(*here, 2)
+                if n == 0:
+                    load_kq(*steps[2])
+                if n == 1:
+                    w_turn(1, 2)
+                    w_turn(1, 3)
+                if n < 2:
+                    w_quant(n)
+                product(*here, 3)
+                for c in sort_at.get(n, []):
+                    ds_sort(*steps[c])
                 if prev:
                     feat_turn(*prev)
                 if 2 <= n < 6:
                     dx(*steps[n - 2])
-                product(*here, 3)
-                if prev:
-                    feat_quant(*prev)
-                for c in new:
-                    ds_sort(*c)
-                if n == 6 or n == 7:
-                    for q in range(2):
-                        x_mix(n - 6, q)
-                    for q in range(2):
-                        x_quant(n - 6, q)
+                for c in x_at.get(n, []):
+                    x_mix(*c)
+                if n == 5 or n == 7:
+                    x_quant(n // 7, 0)
+                    x_quant(n // 7, 1)
             turn(*steps[7])
             turn_sort(*steps[7])
+            feat_quant(*steps[6])
             dx(*steps[4])
             dx(*steps[5])
             tok_mix(1, 0)

@@ -59,26 +59,30 @@ def tile_attention_pa_v_kernel(tc, x, w_qk, b_qk, qk, attn, grad_out, out_0, out
 
         def load_attn(h, t0, t1):
             if t0 == 0:
-                at[h] = work.tile([P, 4, 256], F32, name="at", tag="at", bufs=2)
-                go[h] = work.tile([P, 4, 256], BF16, name="go", tag="go", bufs=2)
+                at[h] = work.tile([P, 4, 256], F32, name="at", tag="at", bufs=1)
+                go[h] = work.tile([P, 4, 256], BF16, name="go", tag="go", bufs=1)
             nc.sync.dma_start(out=at[h][:, t0:t1, :], in_=at_v[h][:, t0:t1, :])
             nc.sync.dma_start(out=go[h][:, t0:t1, :], in_=go_v[h][:, t0:t1, :])
 
-        def load_kq(h, t):
+        def load_kq(h, t, parts=1):
             kq[h, t] = big_tile("kq")
-            for a in range(4):
-                nc.sync.dma_start(
-                    out=kq[h, t][32 * a : 32 * a + 32, :].rearrange("r (q d) -> r q d", d=64),
-                    in_=qk_v[h, t, a],
-                )
+            w = 32 // parts
+            for k in range(parts):
+                for a in range(4):
+                    nc.sync.dma_start(
+                        out=kq[h, t][32 * a : 32 * a + 32, 64 * w * k : 64 * w * (k + 1)].rearrange("r (q d) -> r q d", d=64),
+                        in_=qk_v[h, t, a][:, w * k : w * (k + 1), :],
+                    )
 
-        def load_w(i2):
+        def load_w(i2, parts=1):
             tile = big_tile("wr")
             for k in range(2):
-                nc.sync.dma_start(
-                    out=tile[:, 1024 * k : 1024 * (k + 1)].bitcast(BF16),
-                    in_=w_v[2 * i2 + k],
-                )
+                for j in range(parts):
+                    n = 1024 // parts
+                    nc.sync.dma_start(
+                        out=tile[:, 1024 * k + n * j : 1024 * k + n * (j + 1)].bitcast(BF16),
+                        in_=w_v[2 * i2 + k][:, 2 * n * j : 2 * n * (j + 1)],
+                    )
             wr[i2] = tile
 
         def load_x(h):
@@ -90,6 +94,15 @@ def tile_attention_pa_v_kernel(tc, x, w_qk, b_qk, qk, attn, grad_out, out_0, out
 
         wg = {}
 
+        ws = {}
+
+        def w_sort(c_tile):
+            ws[c_tile] = work.tile([P, 1024], F32, name="ws", tag="ws", bufs=1, align_bytes=64)
+            nc.scalar.copy(
+                out=ws[c_tile][:].rearrange("c (u w) -> c u w", u=2),
+                in_=wr[c_tile // 2][:, 1024 * (c_tile % 2) : 1024 * (c_tile % 2 + 1)].rearrange("c (w u) -> c u w", u=2),
+            )
+
         def w_turn(half, i):
             c_tile = 4 * half + i
             for gp in range(2):
@@ -98,20 +111,22 @@ def tile_attention_pa_v_kernel(tc, x, w_qk, b_qk, qk, attn, grad_out, out_0, out
                 pt = ps_t.tile([P, 4, P], F32, name="pt", tag="pt")
                 for k in range(4):
                     g, u = 2 * gp + k // 2, k % 2
-                    src = wr[c_tile // 2][:, 1024 * (c_tile % 2) + 256 * g + u : 1024 * (c_tile % 2) + 256 * (g + 1) : 2]
+                    if c_tile in ws:
+                        src = ws[c_tile][:, 512 * u + P * g : 512 * u + P * (g + 1)]
+                    else:
+                        src = wr[c_tile // 2][:, 1024 * (c_tile % 2) + 256 * g + u : 1024 * (c_tile % 2) + 256 * (g + 1) : 2]
                     nc.tensor.transpose(pt[:, k, :], src, ident[:])
                 nc.scalar.copy(
                     out=wg[half, gp][:].rearrange("p (g c u) -> p g c u", g=2, u=2)[:, :, P * i : P * (i + 1), :],
                     in_=pt[:].rearrange("p (g u) c -> p g c u", u=2),
                 )
 
-        def w_quant(half):
-            for g in range(4):
-                nc.vector.quantize_mx(
-                    out=w_codes[:, g, 512 * half : 512 * (half + 1)].bitcast(E4M3),
-                    scales=w_scales[:, g, 512 * half : 512 * (half + 1)],
-                    in_=wg[half, g // 2][:, 1024 * (g % 2) : 1024 * (g % 2 + 1)].bitcast(BF16),
-                )
+        def w_quant(half, g):
+            nc.vector.quantize_mx(
+                out=w_codes[:, g, 512 * half : 512 * (half + 1)].bitcast(E4M3),
+                scales=w_scales[:, g, 512 * half : 512 * (half + 1)],
+                in_=wg[half, g // 2][:, 1024 * (g % 2) : 1024 * (g % 2 + 1)].bitcast(BF16),
+            )
 
         xi = {}
 
@@ -164,9 +179,13 @@ def tile_attention_pa_v_kernel(tc, x, w_qk, b_qk, qk, attn, grad_out, out_0, out
             ]
             return ops + [lambda t=t: turn_ds(t) for t in range(t0, t0 + nt)]
 
-        def ds_sort(h, t):
+        def ds_sort(h, t, on_vector=False):
             sr[h, t] = work.tile([P, 32, 16], F32, name="sr", tag="sr", bufs=4)
-            nc.scalar.copy(out=sr[h, t][:], in_=turned_of[h, t][:].rearrange("p j q -> p q j"))
+            src = turned_of[h, t][:].rearrange("p j q -> p q j")
+            if on_vector:
+                nc.vector.tensor_copy(out=sr[h, t][:], in_=src)
+            else:
+                nc.scalar.copy(out=sr[h, t][:], in_=src)
 
         bd = {}
 
@@ -183,7 +202,7 @@ def tile_attention_pa_v_kernel(tc, x, w_qk, b_qk, qk, attn, grad_out, out_0, out
 
         y = {}
 
-        def product(h, t, b):
+        def product(h, t, b, mx=(), every=4):
             if b == 0:
                 y[h, t] = work.tile([P, 1024], F32, name="y", tag="y", bufs=2, align_bytes=64)
             pa = ps_a.tile([P, 8, 64], F32, name="pa", tag="pa")
@@ -196,6 +215,8 @@ def tile_attention_pa_v_kernel(tc, x, w_qk, b_qk, qk, attn, grad_out, out_0, out
                     start=True,
                     stop=True,
                 )
+                if mx and i % every == every - 1:
+                    mx.pop(0)()
             nc.scalar.copy(
                 out=y[h, t][:].bitcast(BF16).rearrange("p (d q e) -> p d q e", d=32, e=2)[:, :, 8 * b : 8 * b + 8, :],
                 in_=pa[:].rearrange("p q (d e) -> p d q e", e=2),
@@ -247,23 +268,35 @@ def tile_attention_pa_v_kernel(tc, x, w_qk, b_qk, qk, attn, grad_out, out_0, out
             )
             fc[h, t] = codes, scales
 
-        def dx(h, t):
+        def dx_ops(h, t, tail=False):
             codes, scales = fc[h, t]
             o0 = work.tile([P, 1024], F32, name="o0", tag="o0", bufs=3)
-            for n in range(2):
-                po = ps_o.tile([P, 512], F32, name="po", tag="po")
-                for g in range(4):
-                    nc.tensor.matmul_mx(
-                        out=po[:],
-                        lhsT=codes[:, P * g : P * (g + 1)].bitcast(E5M2),
-                        lhsT_scale=scales[:, P * g : P * (g + 1)],
-                        rhs=w_codes[:, g, 512 * n : 512 * (n + 1)].bitcast(E4M3),
-                        rhs_scale=w_scales[:, g, 512 * n : 512 * (n + 1)],
-                        start=(g == 0),
-                        stop=(g == 3),
-                    )
-                nc.scalar.copy(out=o0[:, 512 * n : 512 * (n + 1)], in_=po[:])
-            nc.scalar.dma_start(out=o0_v[h, t], in_=o0[:])
+            banks = {}
+
+            def step(n, g):
+                if g == 0 and n == 1 and tail:
+                    banks[n] = ps_a.tile([P, 512], F32, name="pa", tag="pa")
+                elif g == 0:
+                    banks[n] = ps_o.tile([P, 512], F32, name="po", tag="po")
+                nc.tensor.matmul_mx(
+                    out=banks[n][:],
+                    lhsT=codes[:, P * g : P * (g + 1)].bitcast(E5M2),
+                    lhsT_scale=scales[:, P * g : P * (g + 1)],
+                    rhs=w_codes[:, g, 512 * n : 512 * (n + 1)].bitcast(E4M3),
+                    rhs_scale=w_scales[:, g, 512 * n : 512 * (n + 1)],
+                    start=(g == 0),
+                    stop=(g == 3),
+                )
+                if g == 3:
+                    nc.scalar.copy(out=o0[:, 512 * n : 512 * (n + 1)], in_=banks[n][:])
+                    if n == 1:
+                        nc.scalar.dma_start(out=o0_v[h, t], in_=o0[:])
+
+            return [lambda n=n, g=g: step(n, g) for n in range(2) for g in range(4)]
+
+        def dx(h, t):
+            for op in dx_ops(h, t, True):
+                op()
 
         z = {}
 
@@ -284,6 +317,7 @@ def tile_attention_pa_v_kernel(tc, x, w_qk, b_qk, qk, attn, grad_out, out_0, out
 
         def dw(m, gp):
             o1 = big_tile("o1")
+            last = m == 7 and gp == 1
             for k in range(2):
                 g = 2 * gp + k
                 if k == 0:
@@ -306,33 +340,40 @@ def tile_attention_pa_v_kernel(tc, x, w_qk, b_qk, qk, attn, grad_out, out_0, out
                     nc.vector.tensor_copy(out=dst, in_=src)
                 else:
                     nc.scalar.copy(out=dst, in_=src)
-            nc.sync.dma_start(out=out_1[P * m : P * (m + 1), 1024 * gp : 1024 * (gp + 1)], in_=o1[:, 0:1024])
+                if last:
+                    nc.sync.dma_start(out=out_1[P * m : P * (m + 1), 512 * g : 512 * (g + 1)], in_=o1[:, 512 * k : 512 * (k + 1)])
+            if not last:
+                nc.sync.dma_start(out=out_1[P * m : P * (m + 1), 1024 * gp : 1024 * (gp + 1)], in_=o1[:, 0:1024])
 
         steps = [(h, t) for h in range(2) for t in range(4)]
-        ds_at = {0: [(0, 2, 2)], 1: [(1, 0, 2)], 3: [(1, 2, 2)]}
+        ds_at = {0: [(0, 2, 2)], 2: [(1, 0, 2)], 4: [(1, 2, 2)]}
         sort_at = {0: [2], 1: [3], 2: [4, 5], 4: [6, 7]}
-        x_at = {3: [(0, 0), (0, 1)], 4: [(0, 2), (0, 3)], 5: [(1, 0), (1, 1)], 6: [(1, 2), (1, 3)]}
+        dx_at = {4: [0], 5: [1], 6: [2], 7: [3]}
+        x_at = {4: [(0, 0), (0, 1)], 5: [(0, 2), (0, 3)], 6: [(1, 0), (1, 1)], 7: [(1, 2), (1, 3)]}
 
         load_attn(0, 0, 1)
-        load_w(0)
-        load_kq(0, 0)
-        load_attn(0, 1, 4)
+        load_w(0, 2)
         load_w(1)
+        load_attn(0, 1, 2)
+        load_kq(0, 0, 2)
+        load_attn(0, 2, 4)
         load_w(2)
         load_kq(0, 1)
-        load_attn(1, 0, 4)
 
         with tc.manual_schedule():
             for op in ds_ops(0, 0, 1):
                 op()
+            ds_sort(0, 0, True)
             w_turn(0, 0)
-            ds_sort(0, 0)
             w_turn(0, 1)
-            load_w(3)
+            w_turn(0, 2)
+            w_turn(0, 3)
             for c in range(8):
                 spread(0, 0, c)
+            w_sort(4)
             for op in ds_ops(0, 1, 1):
                 op()
+            ds_sort(0, 1, True)
             for n in range(8):
                 here = steps[n]
                 after = steps[n + 1] if n < 7 else None
@@ -340,24 +381,29 @@ def tile_attention_pa_v_kernel(tc, x, w_qk, b_qk, qk, attn, grad_out, out_0, out
                 todo = [op for c in ds_at.get(n, []) for op in ds_ops(*c)]
                 if 0 < n and n + 2 < 8:
                     load_kq(*steps[n + 2])
-                if n == 2 or n == 4:
+                if n == 3 or n == 5:
                     load_x(n // 4)
                 if prev:
                     turn(*prev)
-                product(*here, 0)
+                mx = [op for c in dx_at.get(n, []) for op in dx_ops(*steps[c])]
+                every = 4
+                product(*here, 0, mx, every)
                 if n == 0:
-                    product(*here, 1)
-                    w_turn(0, 2)
-                    ds_sort(0, 1)
+                    product(*here, 1, mx, every)
                 for c in range(8):
                     if c == 2 and prev:
                         turn_sort(*prev)
                     if after:
                         spread(*after, c, n > 1 and c >= 6)
                     if c == 3 and n > 0:
-                        product(*here, 1)
+                        product(*here, 1, mx, every)
                     if todo and c >= 2 and n > 0:
                         todo.pop(0)()
+                for k in range(4):
+                    if todo:
+                        todo.pop(0)()
+                    if n == 0:
+                        w_quant(0, k)
                 for op in todo:
                     op()
                 if 2 <= n:
@@ -368,31 +414,31 @@ def tile_attention_pa_v_kernel(tc, x, w_qk, b_qk, qk, attn, grad_out, out_0, out
                         tok_mix(0, g)
                         tok_quant(0, g - 1)
                     tok_quant(0, 3)
-                if n == 0:
-                    w_turn(0, 3)
-                if n == 1:
-                    w_turn(1, 0)
-                    w_turn(1, 1)
-                product(*here, 2)
+                product(*here, 2, mx, every)
                 if n == 0:
                     load_kq(*steps[2])
+                    load_w(3)
                 if n == 1:
-                    w_turn(1, 2)
-                    w_turn(1, 3)
-                if n < 2:
-                    w_quant(n)
-                product(*here, 3)
+                    load_attn(1, 0, 4)
+                if n < 4:
+                    w_turn(1, n)
+                product(*here, 3, mx, every)
+                if n < 3:
+                    w_sort(5 + n)
                 for c in sort_at.get(n, []):
                     ds_sort(*steps[c])
+                if n == 3:
+                    for g in range(4):
+                        w_quant(1, g)
                 if prev:
                     feat_turn(*prev)
-                if 2 <= n < 6:
-                    dx(*steps[n - 2])
                 for c in x_at.get(n, []):
                     x_mix(*c)
-                if n == 5 or n == 7:
-                    x_quant(n // 7, 0)
-                    x_quant(n // 7, 1)
+                if n == 6:
+                    x_quant(0, 0)
+                    x_quant(0, 1)
+                if n == 7:
+                    x_quant(1, 0)
             turn(*steps[7])
             turn_sort(*steps[7])
             feat_quant(*steps[6])
@@ -402,6 +448,7 @@ def tile_attention_pa_v_kernel(tc, x, w_qk, b_qk, qk, attn, grad_out, out_0, out
             tok_mix(1, 1)
             tok_quant(1, 0)
             tok_quant(1, 1)
+            x_quant(1, 1)
             feat_turn(*steps[7])
             dx(*steps[6])
             feat_quant(*steps[7])

@@ -32,24 +32,24 @@ def tile_attention_pa_v_kernel(tc, x, w_qk, b_qk, qk, attn, grad_out, out_0, out
         big = ctx.enter_context(tc.tile_pool(name="big", bufs=7))
         work = ctx.enter_context(tc.tile_pool(name="work", bufs=2))
         keep = ctx.enter_context(tc.tile_pool(name="keep", bufs=1))
-        ps_a = ctx.enter_context(tc.psum_pool(name="ps_a", bufs=3))
+        ps_a = ctx.enter_context(tc.psum_pool(name="ps_a", bufs=4))
         ps_t = ctx.enter_context(tc.psum_pool(name="ps_t", bufs=2))
-        ps_o = ctx.enter_context(tc.psum_pool(name="ps_o", bufs=3))
+        ps_o = ctx.enter_context(tc.psum_pool(name="ps_o", bufs=2))
 
         ident = const.tile([P, P], F32, name="ident", align_bytes=64)
         make_identity(nc, ident[:])
         blk = const.tile([P, 8], F32, name="blk")
         nc.vector.tensor_reduce(out=blk[:], in_=ident[:].rearrange("p (c x) -> p c x", x=16), axis=AX.X, op=ALU.add)
 
-        w_codes = keep.tile([P, 4, 1024], U32, name="w_codes", align_bytes=64)
-        w_scales = keep.tile([P, 4, 1024], U8, name="w_scales", align_bytes=64)
-        x_codes = keep.tile([P, 2, 1024], U32, name="x_codes", align_bytes=64)
-        x_scales = keep.tile([P, 2, 1024], U8, name="x_scales", align_bytes=64)
-        t_codes = keep.tile([P, 2, 2048], U32, name="t_codes", align_bytes=64)
-        t_scales = keep.tile([P, 2, 2048], U8, name="t_scales", align_bytes=64)
+        w_codes = keep.tile([P, 4, 1024], U32, name="w_codes", align_bytes=256)
+        w_scales = keep.tile([P, 4, 1024], U8, name="w_scales", align_bytes=256)
+        x_codes = keep.tile([P, 2, 1024], U32, name="x_codes", align_bytes=256)
+        x_scales = keep.tile([P, 2, 1024], U8, name="x_scales", align_bytes=256)
+        t_codes = keep.tile([P, 2, 2048], U32, name="t_codes", align_bytes=256)
+        t_scales = keep.tile([P, 2, 2048], U8, name="t_scales", align_bytes=256)
 
         def big_tile(name):
-            return big.tile([P, 2048], F32, name=name, tag="big", align_bytes=64)
+            return big.tile([P, 2048], F32, name=name, tag="big", align_bytes=256)
 
         at = {}
         go = {}
@@ -191,7 +191,7 @@ def tile_attention_pa_v_kernel(tc, x, w_qk, b_qk, qk, attn, grad_out, out_0, out
 
         def spread(h, t, c, on_scalar=False):
             if c == 0:
-                bd[h, t] = work.tile([P, 32, P], F32, name="bd", tag="bd", bufs=2, align_bytes=64)
+                bd[h, t] = work.tile([P, 32, P], F32, name="bd", tag="bd", bufs=2, align_bytes=256)
             a, s = c // 2, c % 2
             out = bd[h, t][:, :, 16 * c : 16 * c + 16]
             mask = blk[:, 2 * a + 1 - s : 2 * a + 2 - s]
@@ -202,14 +202,14 @@ def tile_attention_pa_v_kernel(tc, x, w_qk, b_qk, qk, attn, grad_out, out_0, out
 
         y = {}
 
-        def product(h, t, b, mx=(), every=4):
-            if b == 0:
+        def product(h, t, b2, mx=(), every=4):
+            if b2 == 0:
                 y[h, t] = work.tile([P, 1024], F32, name="y", tag="y", bufs=2, align_bytes=64)
-            pa = ps_a.tile([P, 8, 64], F32, name="pa", tag="pa")
-            for i in range(8):
-                q = 8 * b + i
+            pa = [ps_a.tile([P, 8, 64], F32, name="pa", tag="pa") for k in range(2)]
+            for i in range(16):
+                q = 16 * b2 + 8 * (i % 2) + i // 2
                 nc.tensor.matmul(
-                    pa[:, i, :],
+                    pa[i % 2][:, i // 2, :],
                     lhsT=bd[h, t][:, q, :],
                     rhs=kq[h, t][:, 64 * q : 64 * q + 64],
                     start=True,
@@ -217,10 +217,12 @@ def tile_attention_pa_v_kernel(tc, x, w_qk, b_qk, qk, attn, grad_out, out_0, out
                 )
                 if mx and i % every == every - 1:
                     mx.pop(0)()
-            nc.scalar.copy(
-                out=y[h, t][:].bitcast(BF16).rearrange("p (d q e) -> p d q e", d=32, e=2)[:, :, 8 * b : 8 * b + 8, :],
-                in_=pa[:].rearrange("p q (d e) -> p d q e", e=2),
-            )
+            for k in range(2):
+                b = 2 * b2 + k
+                nc.scalar.copy(
+                    out=y[h, t][:].bitcast(BF16).rearrange("p (d q e) -> p d q e", d=32, e=2)[:, :, 8 * b : 8 * b + 8, :],
+                    in_=pa[k][:].rearrange("p q (d e) -> p d q e", e=2),
+                )
 
         ut = {}
         yt = {}
@@ -259,8 +261,8 @@ def tile_attention_pa_v_kernel(tc, x, w_qk, b_qk, qk, attn, grad_out, out_0, out
         fc = {}
 
         def feat_quant(h, t):
-            codes = work.tile([P, 512], U32, name="f_codes", tag="f_codes", bufs=4, align_bytes=64)
-            scales = work.tile([P, 512], U8, name="f_scales", tag="f_scales", bufs=4, align_bytes=64)
+            codes = work.tile([P, 512], U32, name="f_codes", tag="f_codes", bufs=4, align_bytes=256)
+            scales = work.tile([P, 512], U8, name="f_scales", tag="f_scales", bufs=4, align_bytes=256)
             nc.vector.quantize_mx(
                 out=codes[:].bitcast(E5M2),
                 scales=scales[:],
@@ -274,7 +276,7 @@ def tile_attention_pa_v_kernel(tc, x, w_qk, b_qk, qk, attn, grad_out, out_0, out
             banks = {}
 
             def step(n, g):
-                if g == 0 and n == 1 and tail:
+                if g == 0 and tail:
                     banks[n] = ps_a.tile([P, 512], F32, name="pa", tag="pa")
                 elif g == 0:
                     banks[n] = ps_o.tile([P, 512], F32, name="po", tag="po")
@@ -320,7 +322,7 @@ def tile_attention_pa_v_kernel(tc, x, w_qk, b_qk, qk, attn, grad_out, out_0, out
             last = m == 7 and gp == 1
             for k in range(2):
                 g = 2 * gp + k
-                if k == 0:
+                if (2 * m + k) % 3 == 0:
                     po = ps_o.tile([P, 512], F32, name="po", tag="po")
                 else:
                     po = ps_a.tile([P, 512], F32, name="pa", tag="pa")
@@ -388,15 +390,11 @@ def tile_attention_pa_v_kernel(tc, x, w_qk, b_qk, qk, attn, grad_out, out_0, out
                 mx = [op for c in dx_at.get(n, []) for op in dx_ops(*steps[c])]
                 every = 4
                 product(*here, 0, mx, every)
-                if n == 0:
-                    product(*here, 1, mx, every)
                 for c in range(8):
                     if c == 2 and prev:
                         turn_sort(*prev)
                     if after:
                         spread(*after, c, n > 1 and c >= 6)
-                    if c == 3 and n > 0:
-                        product(*here, 1, mx, every)
                     if todo and c >= 2 and n > 0:
                         todo.pop(0)()
                 for k in range(4):
@@ -414,7 +412,6 @@ def tile_attention_pa_v_kernel(tc, x, w_qk, b_qk, qk, attn, grad_out, out_0, out
                         tok_mix(0, g)
                         tok_quant(0, g - 1)
                     tok_quant(0, 3)
-                product(*here, 2, mx, every)
                 if n == 0:
                     load_kq(*steps[2])
                     load_w(3)
@@ -422,7 +419,7 @@ def tile_attention_pa_v_kernel(tc, x, w_qk, b_qk, qk, attn, grad_out, out_0, out
                     load_attn(1, 0, 4)
                 if n < 4:
                     w_turn(1, n)
-                product(*here, 3, mx, every)
+                product(*here, 1, mx, every)
                 if n < 3:
                     w_sort(5 + n)
                 for c in sort_at.get(n, []):

from contextlib import ExitStack

import concourse.mybir as mybir
from concourse.masks import make_identity

F32 = mybir.dt.float32
BF16 = mybir.dt.bfloat16
U32 = mybir.dt.uint32
U8 = mybir.dt.uint8
E4M3 = mybir.dt.float8_e4m3fn_x4
E5M2 = mybir.dt.float8_e5m2_x4
ALU = mybir.AluOpType
AX = mybir.AxisListType
ACT = mybir.ActivationFunctionType

P = 128
FLOPS = 2 * (2 * 1024 * 1024 * 2048) + 2 * (2 * 1024 * 16 * 16 * 64)


def tile_attention_pa_v_kernel(tc, x, w_qk, b_qk, qk, attn, grad_out, out_0, out_1):
    nc = tc.nc

    x_v = x.rearrange("n t c -> (n t) c").rearrange("(h p j) c -> h p j c", h=2, j=4)
    w_v = w_qk.rearrange("(i c) f -> i c f", c=P)
    qk_v = qk.rearrange("n t f -> (n t) f").rearrange("(h a q t) (r d) -> h t a r q d", h=2, a=4, q=32, t=4, d=64)
    at_v = attn.rearrange("n t h g -> (n t) (h g)").rearrange("(h p t) f -> h p t f", h=2, t=4)
    go_v = grad_out.rearrange("n t h g -> (n t) (h g)").rearrange("(h p t) f -> h p t f", h=2, t=4)
    o0_v = out_0.rearrange("n t c -> (n t) c").rearrange("(h p t) c -> h t p c", h=2, t=4)

    with ExitStack() as ctx:
        const = ctx.enter_context(tc.tile_pool(name="const", bufs=1))
        big = ctx.enter_context(tc.tile_pool(name="big", bufs=7))
        work = ctx.enter_context(tc.tile_pool(name="work", bufs=2))
        keep = ctx.enter_context(tc.tile_pool(name="keep", bufs=1))
        ps_a = ctx.enter_context(tc.psum_pool(name="ps_a", bufs=4))
        ps_t = ctx.enter_context(tc.psum_pool(name="ps_t", bufs=2))
        ps_o = ctx.enter_context(tc.psum_pool(name="ps_o", bufs=2))

        ident = const.tile([P, P], F32, name="ident", align_bytes=64)
        make_identity(nc, ident[:])
        blk = const.tile([P, 8], F32, name="blk")
        nc.vector.tensor_reduce(out=blk[:], in_=ident[:].rearrange("p (c x) -> p c x", x=16), axis=AX.X, op=ALU.add)

        w_codes = keep.tile([P, 4, 1024], U32, name="w_codes", align_bytes=256)
        w_scales = keep.tile([P, 4, 1024], U8, name="w_scales", align_bytes=256)
        x_codes = keep.tile([P, 2, 1024], U32, name="x_codes", align_bytes=256)
        x_scales = keep.tile([P, 2, 1024], U8, name="x_scales", align_bytes=256)
        t_codes = keep.tile([P, 2, 2048], U32, name="t_codes", align_bytes=256)
        t_scales = keep.tile([P, 2, 2048], U8, name="t_scales", align_bytes=256)

        def big_tile(name):
            return big.tile([P, 2048], F32, name=name, tag="big", align_bytes=256)

        at = {}
        go = {}
        kq = {}
        wr = {}
        xr = {}

        def load_attn(h, t0, t1):
            if t0 == 0:
                at[h] = work.tile([P, 4, 256], F32, name="at", tag="at", bufs=1)
                go[h] = work.tile([P, 4, 256], BF16, name="go", tag="go", bufs=1)
            nc.sync.dma_start(out=at[h][:, t0:t1, :], in_=at_v[h][:, t0:t1, :])
            nc.sync.dma_start(out=go[h][:, t0:t1, :], in_=go_v[h][:, t0:t1, :])

        def load_kq(h, t, parts=1):
            kq[h, t] = big_tile("kq")
            w = 32 // parts
            for k in range(parts):
                for a in range(4):
                    nc.sync.dma_start(
                        out=kq[h, t][32 * a : 32 * a + 32, 64 * w * k : 64 * w * (k + 1)].rearrange("r (q d) -> r q d", d=64),
                        in_=qk_v[h, t, a][:, w * k : w * (k + 1), :],
                    )

        def load_w(i2, parts=1):
            tile = big_tile("wr")
            for k in range(2):
                for j in range(parts):
                    n = 1024 // parts
                    nc.sync.dma_start(
                        out=tile[:, 1024 * k + n * j : 1024 * k + n * (j + 1)].bitcast(BF16),
                        in_=w_v[2 * i2 + k][:, 2 * n * j : 2 * n * (j + 1)],
                    )
            wr[i2] = tile

        def load_x(h):
            xr[h] = big_tile("xr")
            nc.sync.dma_start(
                out=xr[h][:].bitcast(BF16).rearrange("p (j c) -> p j c", j=4),
                in_=x_v[h],
            )

        wg = {}

        ws = {}

        def w_sort(c_tile):
            ws[c_tile] = work.tile([P, 1024], F32, name="ws", tag="ws", bufs=1, align_bytes=64)
            nc.scalar.copy(
                out=ws[c_tile][:].rearrange("c (u w) -> c u w", u=2),
                in_=wr[c_tile // 2][:, 1024 * (c_tile % 2) : 1024 * (c_tile % 2 + 1)].rearrange("c (w u) -> c u w", u=2),
            )

        def w_turn(half, i):
            c_tile = 4 * half + i
            for gp in range(2):
                if i == 0:
                    wg[half, gp] = big_tile("wg")
                pt = ps_t.tile([P, 4, P], F32, name="pt", tag="pt")
                for k in range(4):
                    g, u = 2 * gp + k // 2, k % 2
                    if c_tile in ws:
                        src = ws[c_tile][:, 512 * u + P * g : 512 * u + P * (g + 1)]
                    else:
                        src = wr[c_tile // 2][:, 1024 * (c_tile % 2) + 256 * g + u : 1024 * (c_tile % 2) + 256 * (g + 1) : 2]
                    nc.tensor.transpose(pt[:, k, :], src, ident[:])
                nc.scalar.copy(
                    out=wg[half, gp][:].rearrange("p (g c u) -> p g c u", g=2, u=2)[:, :, P * i : P * (i + 1), :],
                    in_=pt[:].rearrange("p (g u) c -> p g c u", u=2),
                )

        def w_quant(half, g):
            nc.vector.quantize_mx(
                out=w_codes[:, g, 512 * half : 512 * (half + 1)].bitcast(E4M3),
                scales=w_scales[:, g, 512 * half : 512 * (half + 1)],
                in_=wg[half, g // 2][:, 1024 * (g % 2) : 1024 * (g % 2 + 1)].bitcast(BF16),
            )

        xi = {}

        def x_mix(h, q):
            if q == 0:
                xi[h] = big_tile("xi")
            nc.scalar.copy(
                out=xi[h][:].bitcast(BF16).rearrange("p (c j) -> p c j", j=4)[:, 256 * q : 256 * (q + 1)],
                in_=xr[h][:].bitcast(BF16).rearrange("p (j c) -> p c j", j=4)[:, 256 * q : 256 * (q + 1)],
            )

        def x_quant(h, q):
            nc.vector.quantize_mx(
                out=x_codes[:, h, 512 * q : 512 * (q + 1)].bitcast(E4M3),
                scales=x_scales[:, h, 512 * q : 512 * (q + 1)],
                in_=xi[h][:, 1024 * q : 1024 * (q + 1)].bitcast(BF16),
            )

        sr = {}
        turned_of = {}

        def ds_ops(h, t0, nt):
            m = 16 * nt
            tmp = work.tile([P, 32, 16], F32, name="tmp", tag="tmp", bufs=2)
            r = work.tile([P, 32], F32, name="r", tag="r", bufs=2)
            df = work.tile([P, 32, 16], F32, name="df", tag="tmp", bufs=2)
            g2 = work.tile([P, 2, 16, 2, 16], F32, name="g2", tag="g2", bufs=1, align_bytes=64)
            for t in range(t0, t0 + nt):
                turned_of[h, t] = work.tile([P, 16, 32], F32, name="turned", tag="turned", bufs=3, align_bytes=64)
            a_s = at[h][:, t0 : t0 + nt, :].rearrange("p t (m g) -> p (t m) g", g=16)
            g_s = go[h][:, t0 : t0 + nt, :].rearrange("p t (m g) -> p (t m) g", g=16)
            nat = g2[:, :nt, :, 1, :]

            def turn_ds(t):
                nc.vector.transpose(
                    out=turned_of[h, t][:].rearrange("p j q -> p (j q)"),
                    in_=g2[:, t - t0].rearrange("p j s x -> p (j s x)"),
                )

            ops = [
                lambda: nc.vector.tensor_tensor(out=tmp[:, :m], in0=g_s, in1=a_s, op=ALU.mult),
                lambda: nc.vector.tensor_reduce(out=r[:, :m], in_=tmp[:, :m], axis=AX.X, op=ALU.add),
                lambda: nc.vector.tensor_tensor(
                    out=df[:, :m], in0=g_s, in1=r[:, :m].unsqueeze(2).to_broadcast([P, m, 16]), op=ALU.subtract
                ),
                lambda: nc.vector.scalar_tensor_tensor(
                    out=nat.rearrange("p t j x -> p (t j) x"), in0=df[:, :m], scalar=0.125, in1=a_s, op0=ALU.mult, op1=ALU.mult
                ),
                lambda: nc.vector.tensor_copy(out=g2[:, :nt, :, 0, :], in_=nat.rearrange("p t j x -> p t x j")),
            ]
            return ops + [lambda t=t: turn_ds(t) for t in range(t0, t0 + nt)]

        def ds_sort(h, t, on_vector=False):
            sr[h, t] = work.tile([P, 32, 16], F32, name="sr", tag="sr", bufs=4)
            src = turned_of[h, t][:].rearrange("p j q -> p q j")
            if on_vector:
                nc.vector.tensor_copy(out=sr[h, t][:], in_=src)
            else:
                nc.scalar.copy(out=sr[h, t][:], in_=src)

        bd = {}

        def spread(h, t, c, on_scalar=False):
            if c == 0:
                bd[h, t] = work.tile([P, 32, P], F32, name="bd", tag="bd", bufs=2, align_bytes=256)
            a, s = c // 2, c % 2
            out = bd[h, t][:, :, 16 * c : 16 * c + 16]
            mask = blk[:, 2 * a + 1 - s : 2 * a + 2 - s]
            if on_scalar:
                nc.scalar.activation(out=out, in_=sr[h, t][:], func=ACT.Copy, scale=mask)
            else:
                nc.vector.tensor_scalar(out=out, in0=sr[h, t][:], scalar1=mask, scalar2=None, op0=ALU.mult)

        y = {}

        def product(h, t, b2, mx=(), every=4):
            if b2 == 0:
                y[h, t] = work.tile([P, 1024], F32, name="y", tag="y", bufs=2, align_bytes=64)
            pa = [ps_a.tile([P, 8, 64], F32, name="pa", tag="pa") for k in range(2)]
            for i in range(16):
                q = 16 * b2 + 8 * (i % 2) + i // 2
                nc.tensor.matmul(
                    pa[i % 2][:, i // 2, :],
                    lhsT=bd[h, t][:, q, :],
                    rhs=kq[h, t][:, 64 * q : 64 * q + 64],
                    start=True,
                    stop=True,
                )
                if mx and i % every == every - 1:
                    mx.pop(0)()
            for k in range(2):
                b = 2 * b2 + k
                nc.scalar.copy(
                    out=y[h, t][:].bitcast(BF16).rearrange("p (d q e) -> p d q e", d=32, e=2)[:, :, 8 * b : 8 * b + 8, :],
                    in_=pa[k][:].rearrange("p q (d e) -> p d q e", e=2),
                )

        ut = {}
        yt = {}

        def turn(h, t):
            if t == 0:
                ut[h] = work.tile([P, 4, 2, 32, 16], F32, name="ut", tag="ut", bufs=1, align_bytes=64)
            yt[h, t] = work.tile([P, 1024], F32, name="yt", tag="yt", bufs=1, align_bytes=64)
            nc.vector.transpose(out=yt[h, t][:], in_=y[h, t][:])

        def turn_sort(h, t):
            for u in range(2):
                nc.vector.tensor_copy(
                    out=ut[h][:, t, u].rearrange("p (mm m) (dd d) -> p mm dd m d", m=4, d=4),
                    in_=yt[h, t][:].rearrange("p (dd d u mm m) -> p u mm dd m d", dd=4, d=4, u=2, m=4)[:, u],
                )

        fq = {}

        def feat_turn(h, t):
            fq[h, t] = work.tile([P, 4, P, 2], F32, name="fq", tag="fq", bufs=2, align_bytes=64)
            for gp in range(2):
                pt = ps_t.tile([P, 4, P], F32, name="pt", tag="pt")
                for k in range(4):
                    g, u = 2 * gp + k // 2, k % 2
                    nc.tensor.transpose(
                        pt[:, k, :],
                        ut[h][:, t, u, 8 * g : 8 * g + 8, :].rearrange("p m d -> p (m d)"),
                        ident[:],
                    )
                nc.scalar.copy(
                    out=fq[h, t][:, 2 * gp : 2 * gp + 2],
                    in_=pt[:].rearrange("p (g u) c -> p g c u", u=2),
                )

        fc = {}

        def feat_quant(h, t):
            codes = work.tile([P, 512], U32, name="f_codes", tag="f_codes", bufs=4, align_bytes=256)
            scales = work.tile([P, 512], U8, name="f_scales", tag="f_scales", bufs=4, align_bytes=256)
            nc.vector.quantize_mx(
                out=codes[:].bitcast(E5M2),
                scales=scales[:],
                in_=fq[h, t][:].rearrange("p g c u -> p (g c u)").bitcast(BF16),
            )
            fc[h, t] = codes, scales

        def dx_ops(h, t, tail=False):
            codes, scales = fc[h, t]
            o0 = work.tile([P, 1024], F32, name="o0", tag="o0", bufs=3)
            banks = {}

            def step(n, g):
                if g == 0 and tail:
                    banks[n] = ps_a.tile([P, 512], F32, name="pa", tag="pa")
                elif g == 0:
                    banks[n] = ps_o.tile([P, 512], F32, name="po", tag="po")
                nc.tensor.matmul_mx(
                    out=banks[n][:],
                    lhsT=codes[:, P * g : P * (g + 1)].bitcast(E5M2),
                    lhsT_scale=scales[:, P * g : P * (g + 1)],
                    rhs=w_codes[:, g, 512 * n : 512 * (n + 1)].bitcast(E4M3),
                    rhs_scale=w_scales[:, g, 512 * n : 512 * (n + 1)],
                    start=(g == 0),
                    stop=(g == 3),
                )
                if g == 3:
                    nc.scalar.copy(out=o0[:, 512 * n : 512 * (n + 1)], in_=banks[n][:])
                    if n == 1:
                        nc.scalar.dma_start(out=o0_v[h, t], in_=o0[:])

            return [lambda n=n, g=g: step(n, g) for n in range(2) for g in range(4)]

        def dx(h, t):
            for op in dx_ops(h, t, True):
                op()

        z = {}

        def tok_mix(h, g):
            z[h, g] = work.tile([P, 2, 256, 4], BF16, name="z", tag="z", bufs=2, align_bytes=64)
            nc.vector.tensor_copy(
                out=z[h, g][:],
                in_=ut[h][:].rearrange("p t u m d -> p (t u m d)").bitcast(BF16)
                .rearrange("p (t u g w) -> p g u w t", t=4, u=2, g=4)[:, g],
            )

        def tok_quant(h, g):
            nc.vector.quantize_mx(
                out=t_codes[:, h, 512 * g : 512 * (g + 1)].bitcast(E5M2),
                scales=t_scales[:, h, 512 * g : 512 * (g + 1)],
                in_=z[h, g][:].rearrange("p u w t -> p (u w t)"),
            )

        def dw(m, gp):
            o1 = big_tile("o1")
            last = m == 7 and gp == 1
            for k in range(2):
                g = 2 * gp + k
                if (2 * m + k) % 3 == 0:
                    po = ps_o.tile([P, 512], F32, name="po", tag="po")
                else:
                    po = ps_a.tile([P, 512], F32, name="pa", tag="pa")
                for h in range(2):
                    nc.tensor.matmul_mx(
                        out=po[:],
                        lhsT=x_codes[:, h, P * m : P * (m + 1)].bitcast(E4M3),
                        lhsT_scale=x_scales[:, h, P * m : P * (m + 1)],
                        rhs=t_codes[:, h, 512 * g : 512 * (g + 1)].bitcast(E5M2),
                        rhs_scale=t_scales[:, h, 512 * g : 512 * (g + 1)],
                        start=(h == 0),
                        stop=(h == 1),
                    )
                dst = o1[:, 512 * k : 512 * (k + 1)].rearrange("p (w u e) -> p w u e", u=2, e=2)
                src = po[:].rearrange("p (u w e) -> p w u e", u=2, e=2)
                if k == 0:
                    nc.vector.tensor_copy(out=dst, in_=src)
                else:
                    nc.scalar.copy(out=dst, in_=src)
                if last:
                    nc.sync.dma_start(out=out_1[P * m : P * (m + 1), 512 * g : 512 * (g + 1)], in_=o1[:, 512 * k : 512 * (k + 1)])
            if not last:
                nc.sync.dma_start(out=out_1[P * m : P * (m + 1), 1024 * gp : 1024 * (gp + 1)], in_=o1[:, 0:1024])

        steps = [(h, t) for h in range(2) for t in range(4)]
        ds_at = {0: [(0, 2, 2)], 2: [(1, 0, 2)], 4: [(1, 2, 2)]}
        sort_at = {0: [2], 1: [3], 2: [4, 5], 4: [6, 7]}
        dx_at = {4: [0], 5: [1], 6: [2], 7: [3]}
        x_at = {4: [(0, 0), (0, 1)], 5: [(0, 2), (0, 3)], 6: [(1, 0), (1, 1)], 7: [(1, 2), (1, 3)]}

        load_attn(0, 0, 1)
        load_w(0, 2)
        load_w(1)
        load_attn(0, 1, 2)
        load_kq(0, 0, 2)
        load_attn(0, 2, 4)
        load_w(2)
        load_kq(0, 1)

        with tc.manual_schedule():
            for op in ds_ops(0, 0, 1):
                op()
            ds_sort(0, 0, True)
            w_turn(0, 0)
            w_turn(0, 1)
            w_turn(0, 2)
            w_turn(0, 3)
            for c in range(8):
                spread(0, 0, c)
            w_sort(4)
            for op in ds_ops(0, 1, 1):
                op()
            ds_sort(0, 1, True)
            for n in range(8):
                here = steps[n]
                after = steps[n + 1] if n < 7 else None
                prev = steps[n - 1] if n > 0 else None
                todo = [op for c in ds_at.get(n, []) for op in ds_ops(*c)]
                if 0 < n and n + 2 < 8:
                    load_kq(*steps[n + 2])
                if n == 3 or n == 5:
                    load_x(n // 4)
                if prev:
                    turn(*prev)
                mx = [op for c in dx_at.get(n, []) for op in dx_ops(*steps[c])]
                every = 4
                product(*here, 0, mx, every)
                for c in range(8):
                    if c == 2 and prev:
                        turn_sort(*prev)
                    if after:
                        spread(*after, c, n > 1 and c >= 6)
                    if todo and c >= 2 and n > 0:
                        todo.pop(0)()
                for k in range(4):
                    if todo:
                        todo.pop(0)()
                    if n == 0:
                        w_quant(0, k)
                for op in todo:
                    op()
                if 2 <= n:
                    feat_quant(*steps[n - 2])
                if n == 4:
                    tok_mix(0, 0)
                    for g in range(1, 4):
                        tok_mix(0, g)
                        tok_quant(0, g - 1)
                    tok_quant(0, 3)
                if n == 0:
                    load_kq(*steps[2])
                    load_w(3)
                if n == 1:
                    load_attn(1, 0, 4)
                if n < 4:
                    w_turn(1, n)
                product(*here, 1, mx, every)
                if n < 3:
                    w_sort(5 + n)
                for c in sort_at.get(n, []):
                    ds_sort(*steps[c])
                if n == 3:
                    for g in range(4):
                        w_quant(1, g)
                if prev:
                    feat_turn(*prev)
                for c in x_at.get(n, []):
                    x_mix(*c)
                if n == 6:
                    x_quant(0, 0)
                    x_quant(0, 1)
                if n == 7:
                    x_quant(1, 0)
            turn(*steps[7])
            turn_sort(*steps[7])
            feat_quant(*steps[6])
            dx(*steps[4])
            dx(*steps[5])
            tok_mix(1, 0)
            tok_mix(1, 1)
            tok_quant(1, 0)
            tok_quant(1, 1)
            x_quant(1, 1)
            feat_turn(*steps[7])
            dx(*steps[6])
            feat_quant(*steps[7])
            dw(0, 0)
            dw(1, 0)
            tok_mix(1, 2)
            tok_mix(1, 3)
            tok_quant(1, 2)
            tok_quant(1, 3)
            dw(2, 0)
            dw(3, 0)
            dx(*steps[7])
            for m in range(4, 8):
                dw(m, 0)
            for m in range(8):
                dw(m, 1)
